import numpy as np
import ml_dtypes


def mxq(x, axis, fmt="e4m3"):
    dtype, down = {"e4m3": (ml_dtypes.float8_e4m3fn, 7), "e5m2": (ml_dtypes.float8_e5m2, 14)}[fmt]
    v = np.moveaxis(np.asarray(x, np.float32).astype(ml_dtypes.bfloat16).astype(np.float64), axis, -1)
    blocks = v.reshape(v.shape[:-1] + (-1, 32))
    amax = np.abs(blocks).max(-1, keepdims=True)
    byte = np.maximum(np.where(amax > 0, np.frexp(amax)[1] - 1 + 127, 0) - down, 1)
    scale = np.exp2(byte - 127.0)
    codes = (blocks / scale).astype(np.float32).astype(dtype).astype(np.float64)
    return np.moveaxis((codes * scale).reshape(v.shape), -1, axis)


WIDE = False


def mx_kscale(k):
    if not WIDE:
        return np.ones(k)
    levels = np.array([10, -10, 5, -5, 0])
    a = np.random.permutation(np.resize(levels, k // 512 * 4)).reshape(k // 512, 4)
    idx = np.arange(k)
    return np.exp2(a[idx // 512, idx % 128 // 32])


BF16 = ml_dtypes.bfloat16


def bf(x):
    return np.asarray(x, np.float32).astype(BF16)


def f64(x):
    return np.asarray(x).astype(np.float64)


B, C, D, MIP, HH, WW = 4, 1024, 128, 32, 16, 32
N = HH * WW


def setup_inputs():
    s = mx_kscale(C)
    g = (B / D) ** 0.25
    return {"q": bf(np.random.standard_normal((B, N, D)) * 1.45 * g),
            "k": bf(np.random.standard_normal((B, D, N)) * 1.6 * g),
            "x": bf(np.random.standard_normal((B, C, HH, WW)) * s[None, :, None, None]),
            "v_w": bf(np.random.standard_normal((C, C)) * 1.5 / np.sqrt(C) * s[:, None] / s[None, :]),
            "v_b": bf(np.random.standard_normal(C) * 0.3 * s),
            "gamma": bf(1.0 + 0.2 * np.random.standard_normal(1))}


def reference(q, k, x, v_w, v_b, gamma):
    xf = f64(x).reshape(B, C, N)
    energy = f64(q) @ f64(k) / np.sqrt(B)
    e = np.exp(energy - energy.max(-1, keepdims=True))
    v = (mxq(f64(v_w), 1, "e4m3") @ mxq(xf, 1, "e4m3")) + f64(v_b)[None, :, None]
    o = (mxq(v, 2, "e4m3") @ mxq(e, 2, "e4m3").transpose(0, 2, 1)) / e.sum(-1)[:, None, :]
    return (f64(gamma)[0] * o + xf).reshape(B, C, HH, WW)

@@ -1,0 +1,317 @@
+from contextlib import ExitStack
+
+import concourse.mybir as mybir
+from concourse.masks import make_identity
+
+F32 = mybir.dt.float32
+BF16 = mybir.dt.bfloat16
+U32 = mybir.dt.uint32
+U8 = mybir.dt.uint8
+FP8X4 = mybir.dt.float8_e4m3fn_x4
+ACT = mybir.ActivationFunctionType
+ALU = mybir.AluOpType
+AX = mybir.AxisListType
+
+B, C, D, N = 4, 1024, 128, 512
+P = 128
+PACK = 4
+K_PASS = P * PACK
+C_PASSES = C // K_PASS
+C_TILES = C // P
+N_TILES = N // P
+PAIR = 2
+ROUNDS = C_TILES // PAIR
+STEPS = B * C_TILES
+
+FLOPS = 2 * B * (N * N * D + C * C * N + C * N * N)
+
+
+def tile_self_attn_pb_kernel(tc, q, k, x, v_w, v_b, gamma, out):
+    nc = tc.nc
+    x_view = x.rearrange("b (r p e) h w -> b p r e (h w)", p=P, e=PAIR)
+    out_view = out.rearrange("b (r p e) h w -> b p r e (h w)", p=P, e=PAIR)
+    w_view = v_w.rearrange("(r p e) k -> p r e k", p=P, e=PAIR)
+
+    with ExitStack() as ctx:
+        keep = ctx.enter_context(tc.tile_pool(name="keep", bufs=1))
+        batch = ctx.enter_context(tc.tile_pool(name="batch", bufs=2))
+        stream = ctx.enter_context(tc.tile_pool(name="stream", bufs=3))
+        outs = ctx.enter_context(tc.tile_pool(name="outs", bufs=8))
+        psum = ctx.enter_context(tc.psum_pool(name="psum", bufs=2))
+
+        gamma_bf = keep.tile([P, 1], BF16)
+        nc.scalar.dma_start(out=gamma_bf[:], in_=gamma.partition_broadcast(P))
+        bias_col = keep.tile([P, ROUNDS, PAIR], BF16)
+        nc.scalar.dma_start(out=bias_col[:], in_=v_b.rearrange("(r p e) -> p r e", p=P, e=PAIR))
+
+        warm = keep.tile([P, 1], F32)
+        nc.vector.memset(warm[:], 0.0)
+        nc.scalar.activation(out=warm[:], in_=warm[:], func=ACT.Exp)
+
+        ident_bf = keep.tile([P, P], BF16)
+        make_identity(nc, ident_bf[:])
+        ident_f32 = keep.tile([P, P], F32)
+        make_identity(nc, ident_f32[:])
+
+        q_sb = keep.tile([P, B, N_TILES, D], BF16)
+        k_sb = keep.tile([P, B, N], BF16)
+        x_raw = keep.tile([P, B, C_TILES, N], BF16)
+        w_raw = keep.tile([P, ROUNDS, PAIR, C], BF16)
+
+        def load_batch(b):
+            nc.sync.dma_start(out=q_sb[:, b], in_=q[b].rearrange("(t p) d -> p t d", p=P))
+            nc.sync.dma_start(out=k_sb[:, b], in_=k[b])
+            nc.sync.dma_start(
+                out=x_raw[:, b].rearrange("p (r e) n -> p r e n", e=PAIR), in_=x_view[b]
+            )
+
+        load_batch(0)
+        for r in range(ROUNDS):
+            nc.sync.dma_start(out=w_raw[:, r], in_=w_view[:, r])
+        for b in range(1, B):
+            load_batch(b)
+
+
+        w_grouped = keep.tile([P, C_PASSES, C * PACK], BF16, align_bytes=64)
+        w_codes = keep.tile([P, C_PASSES, C], U32, align_bytes=64)
+        w_scales = keep.tile([P, C_PASSES, C], U8, align_bytes=64)
+
+        def quantise_weights(r):
+            cols = slice(r * PAIR * P, (r + 1) * PAIR * P)
+            for g in range(C_PASSES):
+                w_ps = psum.tile([P, 2, PAIR, P], F32, tag="tr")
+                for u in range(2):
+                    for e in range(PAIR):
+                        first = (2 * g + u) * P
+                        nc.tensor.transpose(
+                            w_ps[:, u, e, :],
+                            w_raw[:, r, e, :].bitcast(F32)[:, first : first + P],
+                            ident_f32[:],
+                        )
+                words = w_grouped[:, g, :].bitcast(F32)[:, r * 512 : (r + 1) * 512]
+                nc.scalar.copy(
+                    out=words.rearrange("p (c u) -> p c u", u=2),
+                    in_=w_ps[:].rearrange("p u e c -> p (e c) u"),
+                )
+            for g in range(C_PASSES):
+                nc.vector.quantize_mx(
+                    out=w_codes[:, g, cols].bitcast(FP8X4),
+                    scales=w_scales[:, g, cols],
+                    in_=w_grouped[:, g, r * 1024 : (r + 1) * 1024],
+                )
+
+        tiles = {}
+
+        def transpose_queries(b):
+            qT_ps = psum.tile([P, N_TILES, P], BF16, tag="tr")
+            for it in range(N_TILES):
+                nc.tensor.transpose(qT_ps[:, it, :], q_sb[:, b, it, :], ident_bf[:])
+            qT = batch.tile([P, N_TILES, P], BF16)
+            nc.scalar.mul(out=qT[:], in_=qT_ps[:], mul=0.5)
+            tiles[b] = {"qT": qT}
+
+        def scores(b, it):
+            t = tiles[b]
+            if it == 0:
+                t["neg_max"] = batch.tile([P, N_TILES], F32, name="neg_max")
+                t["row_sum"] = batch.tile([P, N_TILES], F32, name="row_sum")
+                t["e_sb"] = batch.tile([P, N_TILES, N], BF16, name="e_sb")
+            energy = psum.tile([P, N], F32, tag="en")
+            nc.tensor.matmul(
+                energy[:], lhsT=t["qT"][:, it, :], rhs=k_sb[:, b, :], start=True, stop=True
+            )
+            nc.vector.tensor_reduce(
+                out=t["neg_max"][:, it : it + 1], in_=energy[:], axis=AX.X, op=ALU.max, negate=True
+            )
+            nc.scalar.activation(
+                out=t["e_sb"][:, it, :],
+                in_=energy[:],
+                func=ACT.Exp,
+                bias=t["neg_max"][:, it : it + 1],
+                scale=1.0,
+                accum_out=t["row_sum"][:, it : it + 1],
+            )
+
+        def transpose_scores(b, it):
+            t = tiles[b]
+            if it == 0:
+                t["e_grouped"] = batch.tile([P, N * PACK], BF16, name="e_grouped", align_bytes=64)
+            eT_ps = psum.tile([P, PACK, P], BF16, tag="tr")
+            for j in range(PACK):
+                nc.tensor.transpose(
+                    eT_ps[:, j, :], t["e_sb"][:, it, j * P : (j + 1) * P], ident_bf[:]
+                )
+            nc.scalar.copy(
+                out=t["e_grouped"][:, it * K_PASS : (it + 1) * K_PASS].rearrange(
+                    "p (i j) -> p i j", j=PACK
+                ),
+                in_=eT_ps[:].rearrange("p j i -> p i j"),
+            )
+
+        def regroup_x(b, piece, copy):
+            if piece == 0:
+                tiles[b]["x_grouped"] = batch.tile(
+                    [P, C_PASSES, N * PACK], BF16, name="x_grouped", align_bytes=64
+                )
+                tiles[b]["x_codes"] = batch.tile(
+                    [P, C_PASSES, N], U32, name="x_codes", align_bytes=64
+                )
+                tiles[b]["x_scales"] = batch.tile(
+                    [P, C_PASSES, N], U8, name="x_scales", align_bytes=64
+                )
+            g, half = divmod(piece, 2)
+            pixels = slice(half * (N // 2), (half + 1) * (N // 2))
+            grouped = tiles[b]["x_grouped"][:, g, half * N * 2 : (half + 1) * N * 2]
+            copy(
+                out=grouped.rearrange("p (c i t) -> p c t i", i=4, t=PACK),
+                in_=x_raw[:, b, g * PACK : (g + 1) * PACK, pixels].rearrange(
+                    "p t (c i) -> p c t i", i=4
+                ),
+            )
+
+        def quantise_x(b, g):
+            t = tiles[b]
+            nc.vector.quantize_mx(
+                out=t["x_codes"][:, g, :].bitcast(FP8X4),
+                scales=t["x_scales"][:, g, :],
+                in_=t["x_grouped"][:, g, :],
+            )
+
+        def spread_gain(b):
+            t = tiles[b]
+            inverse = batch.tile([P, N_TILES], F32)
+            nc.vector.reciprocal(out=inverse[:], in_=t["row_sum"][:])
+            gain = batch.tile([P, N_TILES], F32)
+            nc.vector.tensor_scalar_mul(out=gain[:], in0=inverse[:], scalar1=gamma_f32[:, 0:1])
+            gain_ps = psum.tile([P, N], F32, tag="tr")
+            for it in range(N_TILES):
+                nc.tensor.transpose(
+                    gain_ps[:, it * P : (it + 1) * P],
+                    gain[:, it : it + 1].to_broadcast([P, P]),
+                    ident_f32[:],
+                )
+            gain_row = batch.tile([P, N], F32)
+            nc.scalar.copy(out=gain_row[:], in_=gain_ps[:])
+            t["gain_row"] = gain_row
+
+        def quantise_scores(b):
+            t = tiles[b]
+            t["e_codes"] = batch.tile([P, N], U32, name="e_codes", align_bytes=64)
+            t["e_scales"] = batch.tile([P, N], U8, name="e_scales", align_bytes=64)
+            nc.vector.quantize_mx(
+                out=t["e_codes"][:].bitcast(FP8X4), scales=t["e_scales"][:], in_=t["e_grouped"][:]
+            )
+
+        v_banks, v_words, o_banks = {}, {}, {}
+
+        def values_matmul(n):
+            b, s = divmod(n, C_TILES)
+            cols = slice(s * P, (s + 1) * P)
+            v_ps = psum.tile([P, PACK, P], F32, tag="v")
+            for j in range(PACK):
+                pixels = slice(j * P, (j + 1) * P)
+                for g in range(C_PASSES):
+                    nc.tensor.matmul_mx(
+                        out=v_ps[:, j, :],
+                        lhsT=tiles[b]["x_codes"][:, g, pixels].bitcast(FP8X4),
+                        lhsT_scale=tiles[b]["x_scales"][:, g, pixels],
+                        rhs=w_codes[:, g, cols].bitcast(FP8X4),
+                        rhs_scale=w_scales[:, g, cols],
+                        start=(g == 0),
+                        stop=(g == C_PASSES - 1),
+                    )
+            v_banks[n] = v_ps
+
+        def attend_matmul(n):
+            b = n // C_TILES
+            v_codes, v_scales = v_words[n]
+            o_ps = psum.tile([P, N], F32, tag="o")
+            nc.tensor.matmul_mx(
+                out=o_ps[:],
+                lhsT=v_codes[:].bitcast(FP8X4),
+                lhsT_scale=v_scales[:],
+                rhs=tiles[b]["e_codes"][:].bitcast(FP8X4),
+                rhs_scale=tiles[b]["e_scales"][:],
+                start=True,
+                stop=True,
+            )
+            o_banks[n] = o_ps
+
+        def step(n):
+            if n + 1 < STEPS:
+                values_matmul(n + 1)
+            if 1 <= n <= STEPS:
+                attend_matmul(n - 1)
+            if n < STEPS:
+                v_grouped = stream.tile([P, P, PACK], BF16, align_bytes=64)
+                nc.vector.tensor_tensor(
+                    out=v_grouped[:],
+                    in0=v_banks[n][:].rearrange("p j c -> p c j"),
+                    in1=bias[:, (n % C_TILES) // PAIR, n % PAIR, :].unsqueeze(2).to_broadcast([P, P, PACK]),
+                    op=ALU.add,
+                )
+            if n >= 2:
+                b2, s2 = divmod(n - 2, C_TILES)
+                result = outs.tile([P, N], F32)
+                nc.vector.tensor_tensor(
+                    out=result[:], in0=o_banks[n - 2][:], in1=tiles[b2]["gain_row"][:], op=ALU.mult
+                )
+            if n < STEPS:
+                v_codes = stream.tile([P, P], U32, align_bytes=64)
+                v_scales = stream.tile([P, P], U8, align_bytes=64)
+                nc.vector.quantize_mx(
+                    out=v_codes[:].bitcast(FP8X4),
+                    scales=v_scales[:],
+                    in_=v_grouped[:].rearrange("p c j -> p (c j)"),
+                )
+                v_words[n] = (v_codes, v_scales)
+            if n >= 2:
+                nc.gpsimd.tensor_tensor(
+                    out=result[:], in0=result[:], in1=x_raw[:, b2, s2, :], op=ALU.add
+                )
+                nc.sync.dma_start(out=out_view[b2][:, s2 // PAIR, s2 % PAIR], in_=result[:])
+
+        transpose_queries(0)
+        for it in range(N_TILES):
+            scores(0, it)
+        gamma_f32 = keep.tile([P, 1], F32)
+        nc.vector.tensor_copy(out=gamma_f32[:], in_=gamma_bf[:])
+        bias_ps = psum.tile([P, ROUNDS, PAIR, P], BF16, tag="tr")
+        for r in range(ROUNDS):
+            for e in range(PAIR):
+                nc.tensor.transpose(
+                    bias_ps[:, r, e, :], bias_col[:, r, e : e + 1].to_broadcast([P, P]), ident_bf[:]
+                )
+        bias = keep.tile([P, ROUNDS, PAIR, P], BF16)
+        nc.scalar.copy(out=bias[:], in_=bias_ps[:])
+        for piece in range(2 * C_PASSES):
+            regroup_x(0, piece, nc.vector.tensor_copy)
+        for it in range(N_TILES):
+            transpose_scores(0, it)
+        for g in range(C_PASSES):
+            quantise_x(0, g)
+        quantise_weights(0)
+        spread_gain(0)
+        transpose_queries(1)
+        values_matmul(0)
+
+        for b in range(B):
+            quantise_scores(b)
+            for r in range(ROUNDS):
+                if b == 0 and r + 1 < ROUNDS:
+                    quantise_weights(r + 1)
+                if b + 1 < B:
+                    scores(b + 1, r)
+                    regroup_x(b + 1, r, nc.scalar.copy)
+                step(b * C_TILES + PAIR * r)
+                if b + 1 < B:
+                    transpose_scores(b + 1, r)
+                    if r % 2 == 1:
+                        quantise_x(b + 1, r // 2)
+                step(b * C_TILES + PAIR * r + 1)
+            if b + 1 < B:
+                spread_gain(b + 1)
+            if b + 2 < B:
+                transpose_queries(b + 2)
+        step(STEPS)
+        step(STEPS + 1)

@@ -22,6 +22,7 @@ N_TILES = N // P
 PAIR = 2
 ROUNDS = C_TILES // PAIR
 STEPS = B * C_TILES
+UNITS = B * N_TILES
 
 FLOPS = 2 * B * (N * N * D + C * C * N + C * N * N)
 
@@ -33,6 +34,7 @@ def tile_self_attn_pb_kernel(tc, q, k, x, v_w, v_b, gamma, out):
     w_view = v_w.rearrange("(r p e) k -> p r e k", p=P, e=PAIR)
 
     with ExitStack() as ctx:
+        ctx.enter_context(tc.manual_schedule())
         keep = ctx.enter_context(tc.tile_pool(name="keep", bufs=1))
         batch = ctx.enter_context(tc.tile_pool(name="batch", bufs=2))
         stream = ctx.enter_context(tc.tile_pool(name="stream", bufs=3))
@@ -71,15 +73,13 @@ def tile_self_attn_pb_kernel(tc, q, k, x, v_w, v_b, gamma, out):
         for b in range(1, B):
             load_batch(b)
 
-
         w_grouped = keep.tile([P, C_PASSES, C * PACK], BF16, align_bytes=64)
         w_codes = keep.tile([P, C_PASSES, C], U32, align_bytes=64)
         w_scales = keep.tile([P, C_PASSES, C], U8, align_bytes=64)
 
-        def quantise_weights(r):
-            cols = slice(r * PAIR * P, (r + 1) * PAIR * P)
+        def transpose_weights(r):
             for g in range(C_PASSES):
-                w_ps = psum.tile([P, 2, PAIR, P], F32, tag="tr")
+                w_ps = psum.tile([P, 2, PAIR, P], F32, tag=("v", "o")[g])
                 for u in range(2):
                     for e in range(PAIR):
                         first = (2 * g + u) * P
@@ -88,21 +88,27 @@ def tile_self_attn_pb_kernel(tc, q, k, x, v_w, v_b, gamma, out):
                             w_raw[:, r, e, :].bitcast(F32)[:, first : first + P],
                             ident_f32[:],
                         )
-                words = w_grouped[:, g, :].bitcast(F32)[:, r * 512 : (r + 1) * 512]
+                words = w_grouped[:, g, :].bitcast(F32)[:, r * N : (r + 1) * N]
                 nc.scalar.copy(
                     out=words.rearrange("p (c u) -> p c u", u=2),
                     in_=w_ps[:].rearrange("p u e c -> p (e c) u"),
                 )
+
+        def quantise_weights(r):
+            cols = slice(r * PAIR * P, (r + 1) * PAIR * P)
             for g in range(C_PASSES):
                 nc.vector.quantize_mx(
                     out=w_codes[:, g, cols].bitcast(FP8X4),
                     scales=w_scales[:, g, cols],
-                    in_=w_grouped[:, g, r * 1024 : (r + 1) * 1024],
+                    in_=w_grouped[:, g, r * PAIR * K_PASS : (r + 1) * PAIR * K_PASS],
                 )
 
         tiles = {}
+        energies = {}
 
         def transpose_queries(b):
+            if b >= B:
+                return
             qT_ps = psum.tile([P, N_TILES, P], BF16, tag="tr")
             for it in range(N_TILES):
                 nc.tensor.transpose(qT_ps[:, it, :], q_sb[:, b, it, :], ident_bf[:])
@@ -110,29 +116,45 @@ def tile_self_attn_pb_kernel(tc, q, k, x, v_w, v_b, gamma, out):
             nc.scalar.mul(out=qT[:], in_=qT_ps[:], mul=0.5)
             tiles[b] = {"qT": qT}
 
-        def scores(b, it):
+        def energy_matmul(u):
+            if u >= UNITS:
+                return
+            b, it = divmod(u, N_TILES)
+            energy = psum.tile([P, N], F32, tag="en")
+            nc.tensor.matmul(
+                energy[:], lhsT=tiles[b]["qT"][:, it, :], rhs=k_sb[:, b, :], start=True, stop=True
+            )
+            energies[u] = energy
+
+        def softmax(u):
+            if u >= UNITS:
+                return
+            b, it = divmod(u, N_TILES)
             t = tiles[b]
             if it == 0:
                 t["neg_max"] = batch.tile([P, N_TILES], F32, name="neg_max")
                 t["row_sum"] = batch.tile([P, N_TILES], F32, name="row_sum")
                 t["e_sb"] = batch.tile([P, N_TILES, N], BF16, name="e_sb")
-            energy = psum.tile([P, N], F32, tag="en")
-            nc.tensor.matmul(
-                energy[:], lhsT=t["qT"][:, it, :], rhs=k_sb[:, b, :], start=True, stop=True
-            )
             nc.vector.tensor_reduce(
-                out=t["neg_max"][:, it : it + 1], in_=energy[:], axis=AX.X, op=ALU.max, negate=True
+                out=t["neg_max"][:, it : it + 1],
+                in_=energies[u][:],
+                axis=AX.X,
+                op=ALU.max,
+                negate=True,
             )
             nc.scalar.activation(
                 out=t["e_sb"][:, it, :],
-                in_=energy[:],
+                in_=energies[u][:],
                 func=ACT.Exp,
                 bias=t["neg_max"][:, it : it + 1],
                 scale=1.0,
                 accum_out=t["row_sum"][:, it : it + 1],
             )
 
-        def transpose_scores(b, it):
+        def transpose_scores(u):
+            if u >= UNITS:
+                return
+            b, it = divmod(u, N_TILES)
             t = tiles[b]
             if it == 0:
                 t["e_grouped"] = batch.tile([P, N * PACK], BF16, name="e_grouped", align_bytes=64)
@@ -148,52 +170,6 @@ def tile_self_attn_pb_kernel(tc, q, k, x, v_w, v_b, gamma, out):
                 in_=eT_ps[:].rearrange("p j i -> p i j"),
             )
 
-        def regroup_x(b, piece, copy):
-            if piece == 0:
-                tiles[b]["x_grouped"] = batch.tile(
-                    [P, C_PASSES, N * PACK], BF16, name="x_grouped", align_bytes=64
-                )
-                tiles[b]["x_codes"] = batch.tile(
-                    [P, C_PASSES, N], U32, name="x_codes", align_bytes=64
-                )
-                tiles[b]["x_scales"] = batch.tile(
-                    [P, C_PASSES, N], U8, name="x_scales", align_bytes=64
-                )
-            g, half = divmod(piece, 2)
-            pixels = slice(half * (N // 2), (half + 1) * (N // 2))
-            grouped = tiles[b]["x_grouped"][:, g, half * N * 2 : (half + 1) * N * 2]
-            copy(
-                out=grouped.rearrange("p (c i t) -> p c t i", i=4, t=PACK),
-                in_=x_raw[:, b, g * PACK : (g + 1) * PACK, pixels].rearrange(
-                    "p t (c i) -> p c t i", i=4
-                ),
-            )
-
-        def quantise_x(b, g):
-            t = tiles[b]
-            nc.vector.quantize_mx(
-                out=t["x_codes"][:, g, :].bitcast(FP8X4),
-                scales=t["x_scales"][:, g, :],
-                in_=t["x_grouped"][:, g, :],
-            )
-
-        def spread_gain(b):
-            t = tiles[b]
-            inverse = batch.tile([P, N_TILES], F32)
-            nc.vector.reciprocal(out=inverse[:], in_=t["row_sum"][:])
-            gain = batch.tile([P, N_TILES], F32)
-            nc.vector.tensor_scalar_mul(out=gain[:], in0=inverse[:], scalar1=gamma_f32[:, 0:1])
-            gain_ps = psum.tile([P, N], F32, tag="tr")
-            for it in range(N_TILES):
-                nc.tensor.transpose(
-                    gain_ps[:, it * P : (it + 1) * P],
-                    gain[:, it : it + 1].to_broadcast([P, P]),
-                    ident_f32[:],
-                )
-            gain_row = batch.tile([P, N], F32)
-            nc.scalar.copy(out=gain_row[:], in_=gain_ps[:])
-            t["gain_row"] = gain_row
-
         def quantise_scores(b):
             t = tiles[b]
             t["e_codes"] = batch.tile([P, N], U32, name="e_codes", align_bytes=64)
@@ -202,9 +178,65 @@ def tile_self_attn_pb_kernel(tc, q, k, x, v_w, v_b, gamma, out):
                 out=t["e_codes"][:].bitcast(FP8X4), scales=t["e_scales"][:], in_=t["e_grouped"][:]
             )
 
-        v_banks, v_words, o_banks = {}, {}, {}
+        def regroup_x(u, copy):
+            if u >= UNITS:
+                return
+            b, piece = divmod(u, N_TILES)
+            t = tiles[b]
+            if piece == 0:
+                t["x_grouped"] = batch.tile(
+                    [P, C_PASSES, N * PACK], BF16, name="x_grouped", align_bytes=64
+                )
+                t["x_codes"] = batch.tile([P, C_PASSES, N], U32, name="x_codes", align_bytes=64)
+                t["x_scales"] = batch.tile([P, C_PASSES, N], U8, name="x_scales", align_bytes=64)
+            g, half = divmod(piece, 2)
+            pixels = slice(half * (N // 2), (half + 1) * (N // 2))
+            grouped = t["x_grouped"][:, g, half * N * 2 : (half + 1) * N * 2]
+            copy(
+                out=grouped.rearrange("p (c i t) -> p c t i", i=4, t=PACK),
+                in_=x_raw[:, b, g * PACK : (g + 1) * PACK, pixels].rearrange(
+                    "p t (c i) -> p c t i", i=4
+                ),
+            )
+
+        def quantise_x(b, g):
+            if b >= B:
+                return
+            t = tiles[b]
+            nc.vector.quantize_mx(
+                out=t["x_codes"][:, g, :].bitcast(FP8X4),
+                scales=t["x_scales"][:, g, :],
+                in_=t["x_grouped"][:, g, :],
+            )
+
+        def gain_column(b):
+            if b >= B:
+                return
+            inverse = batch.tile([P, N_TILES], F32)
+            nc.vector.reciprocal(out=inverse[:], in_=tiles[b]["row_sum"][:])
+            gain = batch.tile([P, N_TILES], F32)
+            nc.vector.tensor_scalar_mul(out=gain[:], in0=inverse[:], scalar1=gamma_f32[:, 0:1])
+            tiles[b]["gain"] = gain
+
+        def spread_gain(b):
+            if b >= B:
+                return
+            gain_ps = psum.tile([P, N], F32, tag="tr")
+            for it in range(N_TILES):
+                nc.tensor.transpose(
+                    gain_ps[:, it * P : (it + 1) * P],
+                    tiles[b]["gain"][:, it : it + 1].to_broadcast([P, P]),
+                    ident_f32[:],
+                )
+            gain_row = batch.tile([P, N], F32)
+            nc.scalar.copy(out=gain_row[:], in_=gain_ps[:])
+            tiles[b]["gain_row"] = gain_row
+
+        v_banks, v_groups, v_words, o_banks, results = {}, {}, {}, {}, {}
 
         def values_matmul(n):
+            if n >= STEPS:
+                return
             b, s = divmod(n, C_TILES)
             cols = slice(s * P, (s + 1) * P)
             v_ps = psum.tile([P, PACK, P], F32, tag="v")
@@ -222,7 +254,34 @@ def tile_self_attn_pb_kernel(tc, q, k, x, v_w, v_b, gamma, out):
                     )
             v_banks[n] = v_ps
 
+        def add_bias(n):
+            if n >= STEPS:
+                return
+            s = n % C_TILES
+            v_grouped = stream.tile([P, P, PACK], BF16, align_bytes=64)
+            nc.vector.tensor_tensor(
+                out=v_grouped[:],
+                in0=v_banks[n][:].rearrange("p j c -> p c j"),
+                in1=bias[:, s // PAIR, s % PAIR, :].unsqueeze(2).to_broadcast([P, P, PACK]),
+                op=ALU.add,
+            )
+            v_groups[n] = v_grouped
+
+        def quantise_values(n):
+            if n >= STEPS:
+                return
+            v_codes = stream.tile([P, P], U32, align_bytes=64)
+            v_scales = stream.tile([P, P], U8, align_bytes=64)
+            nc.vector.quantize_mx(
+                out=v_codes[:].bitcast(FP8X4),
+                scales=v_scales[:],
+                in_=v_groups[n][:].rearrange("p c j -> p (c j)"),
+            )
+            v_words[n] = (v_codes, v_scales)
+
         def attend_matmul(n):
+            if n < 0 or n >= STEPS:
+                return
             b = n // C_TILES
             v_codes, v_scales = v_words[n]
             o_ps = psum.tile([P, N], F32, tag="o")
@@ -237,43 +296,42 @@ def tile_self_attn_pb_kernel(tc, q, k, x, v_w, v_b, gamma, out):
             )
             o_banks[n] = o_ps
 
-        def step(n):
-            if n + 1 < STEPS:
-                values_matmul(n + 1)
-            if 1 <= n <= STEPS:
-                attend_matmul(n - 1)
-            if n < STEPS:
-                v_grouped = stream.tile([P, P, PACK], BF16, align_bytes=64)
-                nc.vector.tensor_tensor(
-                    out=v_grouped[:],
-                    in0=v_banks[n][:].rearrange("p j c -> p c j"),
-                    in1=bias[:, (n % C_TILES) // PAIR, n % PAIR, :].unsqueeze(2).to_broadcast([P, P, PACK]),
-                    op=ALU.add,
-                )
-            if n >= 2:
-                b2, s2 = divmod(n - 2, C_TILES)
-                result = outs.tile([P, N], F32)
-                nc.vector.tensor_tensor(
-                    out=result[:], in0=o_banks[n - 2][:], in1=tiles[b2]["gain_row"][:], op=ALU.mult
-                )
-            if n < STEPS:
-                v_codes = stream.tile([P, P], U32, align_bytes=64)
-                v_scales = stream.tile([P, P], U8, align_bytes=64)
-                nc.vector.quantize_mx(
-                    out=v_codes[:].bitcast(FP8X4),
-                    scales=v_scales[:],
-                    in_=v_grouped[:].rearrange("p c j -> p (c j)"),
-                )
-                v_words[n] = (v_codes, v_scales)
-            if n >= 2:
-                nc.gpsimd.tensor_tensor(
-                    out=result[:], in0=result[:], in1=x_raw[:, b2, s2, :], op=ALU.add
-                )
-                nc.sync.dma_start(out=out_view[b2][:, s2 // PAIR, s2 % PAIR], in_=result[:])
+        def scale(n):
+            if n < 0 or n >= STEPS:
+                return
+            result = outs.tile([P, N], F32)
+            nc.vector.tensor_tensor(
+                out=result[:],
+                in0=o_banks[n][:],
+                in1=tiles[n // C_TILES]["gain_row"][:],
+                op=ALU.mult,
+            )
+            results[n] = result
+
+        def add_residual(n):
+            if n < 0 or n >= STEPS:
+                return
+            b, s = divmod(n, C_TILES)
+            engine = nc.gpsimd if n < STEPS - 2 else nc.vector
+            engine.tensor_tensor(
+                out=results[n][:], in0=results[n][:], in1=x_raw[:, b, s, :], op=ALU.add
+            )
+            nc.sync.dma_start(out=out_view[b][:, s // PAIR, s % PAIR], in_=results[n][:])
+
+        def front(n):
+            values_matmul(n + 1)
+            attend_matmul(n - 1)
+            add_bias(n)
+
+        def back(n):
+            scale(n - 2)
+            quantise_values(n)
+            add_residual(n - 2)
 
         transpose_queries(0)
-        for it in range(N_TILES):
-            scores(0, it)
+        for u in range(N_TILES):
+            energy_matmul(u)
+            softmax(u)
         gamma_f32 = keep.tile([P, 1], F32)
         nc.vector.tensor_copy(out=gamma_f32[:], in_=gamma_bf[:])
         bias_ps = psum.tile([P, ROUNDS, PAIR, P], BF16, tag="tr")
@@ -284,34 +342,42 @@ def tile_self_attn_pb_kernel(tc, q, k, x, v_w, v_b, gamma, out):
                 )
         bias = keep.tile([P, ROUNDS, PAIR, P], BF16)
         nc.scalar.copy(out=bias[:], in_=bias_ps[:])
-        for piece in range(2 * C_PASSES):
-            regroup_x(0, piece, nc.vector.tensor_copy)
-        for it in range(N_TILES):
-            transpose_scores(0, it)
+        for u in range(N_TILES):
+            regroup_x(u, nc.vector.tensor_copy)
         for g in range(C_PASSES):
             quantise_x(0, g)
-        quantise_weights(0)
+        gain_column(0)
+        for r in range(ROUNDS):
+            transpose_weights(r)
+            transpose_scores(r)
+            quantise_weights(r)
         spread_gain(0)
         transpose_queries(1)
+        energy_matmul(N_TILES)
         values_matmul(0)
+        softmax(N_TILES)
 
-        for b in range(B):
-            quantise_scores(b)
-            for r in range(ROUNDS):
-                if b == 0 and r + 1 < ROUNDS:
-                    quantise_weights(r + 1)
-                if b + 1 < B:
-                    scores(b + 1, r)
-                    regroup_x(b + 1, r, nc.scalar.copy)
-                step(b * C_TILES + PAIR * r)
-                if b + 1 < B:
-                    transpose_scores(b + 1, r)
-                    if r % 2 == 1:
-                        quantise_x(b + 1, r // 2)
-                step(b * C_TILES + PAIR * r + 1)
-            if b + 1 < B:
+        for i in range(B * ROUNDS):
+            b, r = divmod(i, ROUNDS)
+            n = PAIR * i
+            if r == 0:
+                quantise_scores(b)
+            energy_matmul(i + N_TILES + 1)
+            regroup_x(i + N_TILES, nc.scalar.copy)
+            front(n)
+            softmax(i + N_TILES + 1)
+            back(n)
+            if r == ROUNDS - 1:
+                gain_column(b + 1)
+            transpose_scores(i + N_TILES)
+            if r == ROUNDS - 1:
                 spread_gain(b + 1)
-            if b + 2 < B:
+            if r == ROUNDS - 2:
                 transpose_queries(b + 2)
-        step(STEPS)
-        step(STEPS + 1)
+            if r % 2 == 1:
+                quantise_x(b + 1, r // 2)
+            front(n + 1)
+            back(n + 1)
+        for n in range(STEPS, STEPS + 2):
+            front(n)
+            back(n)

@@ -60,18 +60,24 @@ def tile_self_attn_pb_kernel(tc, q, k, x, v_w, v_b, gamma, out):
         x_raw = keep.tile([P, B, C_TILES, N], BF16)
         w_raw = keep.tile([P, ROUNDS, PAIR, C], BF16)
 
-        def load_batch(b):
+        def load_qk(b):
             nc.sync.dma_start(out=q_sb[:, b], in_=q[b].rearrange("(t p) d -> p t d", p=P))
             nc.sync.dma_start(out=k_sb[:, b], in_=k[b])
+
+        def load_x(b):
             nc.sync.dma_start(
                 out=x_raw[:, b].rearrange("p (r e) n -> p r e n", e=PAIR), in_=x_view[b]
             )
 
-        load_batch(0)
+        load_qk(0)
+        load_qk(1)
+        load_x(0)
         for r in range(ROUNDS):
             nc.sync.dma_start(out=w_raw[:, r], in_=w_view[:, r])
-        for b in range(1, B):
-            load_batch(b)
+        load_x(1)
+        for b in range(2, B):
+            load_qk(b)
+            load_x(b)
 
         w_grouped = keep.tile([P, C_PASSES, C * PACK], BF16, align_bytes=64)
         w_codes = keep.tile([P, C_PASSES, C], U32, align_bytes=64)
@@ -209,14 +215,12 @@ def tile_self_attn_pb_kernel(tc, q, k, x, v_w, v_b, gamma, out):
                 in_=t["x_grouped"][:, g, :],
             )
 
-        def gain_column(b):
+        def invert_sums(b):
             if b >= B:
                 return
             inverse = batch.tile([P, N_TILES], F32)
             nc.vector.reciprocal(out=inverse[:], in_=tiles[b]["row_sum"][:])
-            gain = batch.tile([P, N_TILES], F32)
-            nc.vector.tensor_scalar_mul(out=gain[:], in0=inverse[:], scalar1=gamma_f32[:, 0:1])
-            tiles[b]["gain"] = gain
+            tiles[b]["inverse"] = inverse
 
         def spread_gain(b):
             if b >= B:
@@ -225,11 +229,13 @@ def tile_self_attn_pb_kernel(tc, q, k, x, v_w, v_b, gamma, out):
             for it in range(N_TILES):
                 nc.tensor.transpose(
                     gain_ps[:, it * P : (it + 1) * P],
-                    tiles[b]["gain"][:, it : it + 1].to_broadcast([P, P]),
+                    tiles[b]["inverse"][:, it : it + 1].to_broadcast([P, P]),
                     ident_f32[:],
                 )
             gain_row = batch.tile([P, N], F32)
-            nc.scalar.copy(out=gain_row[:], in_=gain_ps[:])
+            nc.scalar.activation(
+                out=gain_row[:], in_=gain_ps[:], func=ACT.Copy, scale=gamma_f32[:, 0:1]
+            )
             tiles[b]["gain_row"] = gain_row
 
         v_banks, v_groups, v_words, o_banks, results = {}, {}, {}, {}, {}
@@ -323,12 +329,8 @@ def tile_self_attn_pb_kernel(tc, q, k, x, v_w, v_b, gamma, out):
             attend_matmul(n - 1)
             add_bias(n)
 
-        def back(n):
-            scale(n - 2)
-            quantise_values(n)
-            add_residual(n - 2)
-
         transpose_queries(0)
+        transpose_queries(1)
         for u in range(N_TILES):
             energy_matmul(u)
             softmax(u)
@@ -346,38 +348,44 @@ def tile_self_attn_pb_kernel(tc, q, k, x, v_w, v_b, gamma, out):
             regroup_x(u, nc.vector.tensor_copy)
         for g in range(C_PASSES):
             quantise_x(0, g)
-        gain_column(0)
+        invert_sums(0)
         for r in range(ROUNDS):
             transpose_weights(r)
             transpose_scores(r)
             quantise_weights(r)
-        spread_gain(0)
-        transpose_queries(1)
         energy_matmul(N_TILES)
+        spread_gain(0)
         values_matmul(0)
         softmax(N_TILES)
+        quantise_scores(0)
 
         for i in range(B * ROUNDS):
             b, r = divmod(i, ROUNDS)
             n = PAIR * i
-            if r == 0:
-                quantise_scores(b)
             energy_matmul(i + N_TILES + 1)
             regroup_x(i + N_TILES, nc.scalar.copy)
             front(n)
             softmax(i + N_TILES + 1)
-            back(n)
+            scale(n - 2)
+            quantise_values(n)
+            if r % 2 == 1:
+                quantise_x(b + 1, r // 2)
+            add_residual(n - 2)
+
             if r == ROUNDS - 1:
-                gain_column(b + 1)
+                invert_sums(b + 1)
             transpose_scores(i + N_TILES)
             if r == ROUNDS - 1:
                 spread_gain(b + 1)
             if r == ROUNDS - 2:
                 transpose_queries(b + 2)
-            if r % 2 == 1:
-                quantise_x(b + 1, r // 2)
             front(n + 1)
-            back(n + 1)
-        for n in range(STEPS, STEPS + 2):
-            front(n)
-            back(n)
+            scale(n - 1)
+            quantise_values(n + 1)
+            if r == ROUNDS - 1 and b + 1 < B:
+                quantise_scores(b + 1)
+            add_residual(n - 1)
+        attend_matmul(STEPS - 1)
+        for n in range(STEPS - 2, STEPS):
+            scale(n)
+            add_residual(n)

@@ -21,7 +21,7 @@ C_TILES = C // P
 N_TILES = N // P
 PAIR = 2
 ROUNDS = C_TILES // PAIR
-STEPS = B * C_TILES
+TURNS = B * ROUNDS
 UNITS = B * N_TILES
 
 FLOPS = 2 * B * (N * N * D + C * C * N + C * N * N)
@@ -38,7 +38,7 @@ def tile_self_attn_pb_kernel(tc, q, k, x, v_w, v_b, gamma, out):
         keep = ctx.enter_context(tc.tile_pool(name="keep", bufs=1))
         batch = ctx.enter_context(tc.tile_pool(name="batch", bufs=2))
         stream = ctx.enter_context(tc.tile_pool(name="stream", bufs=3))
-        outs = ctx.enter_context(tc.tile_pool(name="outs", bufs=8))
+        outs = ctx.enter_context(tc.tile_pool(name="outs", bufs=4))
         psum = ctx.enter_context(tc.psum_pool(name="psum", bufs=2))
 
         gamma_bf = keep.tile([P, 1], BF16)
@@ -64,53 +64,66 @@ def tile_self_attn_pb_kernel(tc, q, k, x, v_w, v_b, gamma, out):
             nc.sync.dma_start(out=q_sb[:, b], in_=q[b].rearrange("(t p) d -> p t d", p=P))
             nc.sync.dma_start(out=k_sb[:, b], in_=k[b])
 
-        def load_x(b):
+        def load_x(b, g):
+            halves = slice(2 * g, 2 * g + 2)
             nc.sync.dma_start(
-                out=x_raw[:, b].rearrange("p (r e) n -> p r e n", e=PAIR), in_=x_view[b]
+                out=x_raw[:, b].rearrange("p (r e) n -> p r e n", e=PAIR)[:, halves],
+                in_=x_view[b][:, halves],
             )
 
-        load_qk(0)
-        load_qk(1)
-        load_x(0)
-        for r in range(ROUNDS):
+        def load_w(r):
             nc.sync.dma_start(out=w_raw[:, r], in_=w_view[:, r])
-        load_x(1)
+
+        load_qk(0)
+        for g in range(C_PASSES):
+            load_x(0, g)
+        load_w(0)
+        load_qk(1)
+        for r in range(1, ROUNDS):
+            load_w(r)
+        for g in range(C_PASSES):
+            load_x(1, g)
         for b in range(2, B):
             load_qk(b)
-            load_x(b)
+            for g in range(C_PASSES):
+                load_x(b, g)
 
         w_grouped = keep.tile([P, C_PASSES, C * PACK], BF16, align_bytes=64)
         w_codes = keep.tile([P, C_PASSES, C], U32, align_bytes=64)
         w_scales = keep.tile([P, C_PASSES, C], U8, align_bytes=64)
 
-        def transpose_weights(r):
-            for g in range(C_PASSES):
-                w_ps = psum.tile([P, 2, PAIR, P], F32, tag=("v", "o")[g])
-                for u in range(2):
-                    for e in range(PAIR):
-                        first = (2 * g + u) * P
-                        nc.tensor.transpose(
-                            w_ps[:, u, e, :],
-                            w_raw[:, r, e, :].bitcast(F32)[:, first : first + P],
-                            ident_f32[:],
-                        )
-                words = w_grouped[:, g, :].bitcast(F32)[:, r * N : (r + 1) * N]
-                nc.scalar.copy(
-                    out=words.rearrange("p (c u) -> p c u", u=2),
-                    in_=w_ps[:].rearrange("p u e c -> p (e c) u"),
-                )
+        w_banks = {}
 
-        def quantise_weights(r):
+        def transpose_weights(r, g):
+            w_ps = psum.tile([P, 2, PAIR, P], F32, tag="v" if g == 0 and r < ROUNDS - 1 else "o")
+            for u in range(2):
+                for e in range(PAIR):
+                    first = (2 * g + u) * P
+                    nc.tensor.transpose(
+                        w_ps[:, u, e, :],
+                        w_raw[:, r, e, :].bitcast(F32)[:, first : first + P],
+                        ident_f32[:],
+                    )
+            w_banks[r, g] = w_ps
+
+        def group_weights(r, g, copy):
+            words = w_grouped[:, g, :].bitcast(F32)[:, r * N : (r + 1) * N]
+            copy(
+                out=words.rearrange("p (c u) -> p c u", u=2),
+                in_=w_banks[r, g][:].rearrange("p u e c -> p (e c) u"),
+            )
+
+        def quantise_weights(r, g):
             cols = slice(r * PAIR * P, (r + 1) * PAIR * P)
-            for g in range(C_PASSES):
-                nc.vector.quantize_mx(
-                    out=w_codes[:, g, cols].bitcast(FP8X4),
-                    scales=w_scales[:, g, cols],
-                    in_=w_grouped[:, g, r * PAIR * K_PASS : (r + 1) * PAIR * K_PASS],
-                )
+            nc.vector.quantize_mx(
+                out=w_codes[:, g, cols].bitcast(FP8X4),
+                scales=w_scales[:, g, cols],
+                in_=w_grouped[:, g, r * PAIR * K_PASS : (r + 1) * PAIR * K_PASS],
+            )
 
         tiles = {}
         energies = {}
+        score_banks = {}
 
         def transpose_queries(b):
             if b >= B:
@@ -149,8 +162,8 @@ def tile_self_attn_pb_kernel(tc, q, k, x, v_w, v_b, gamma, out):
                 negate=True,
             )
             nc.scalar.activation(
-                out=t["e_sb"][:, it, :],
-                in_=energies[u][:],
+                out=t["e_sb"][:, it, :].rearrange("q (u p e) -> q u p e", u=2, e=2),
+                in_=energies[u][:].rearrange("q (u e p) -> q u p e", u=2, e=2),
                 func=ACT.Exp,
                 bias=t["neg_max"][:, it : it + 1],
                 scale=1.0,
@@ -164,16 +177,23 @@ def tile_self_attn_pb_kernel(tc, q, k, x, v_w, v_b, gamma, out):
             t = tiles[b]
             if it == 0:
                 t["e_grouped"] = batch.tile([P, N * PACK], BF16, name="e_grouped", align_bytes=64)
-            eT_ps = psum.tile([P, PACK, P], BF16, tag="tr")
-            for j in range(PACK):
+            eT_ps = psum.tile([P, 2, P], F32, tag="tr")
+            for h in range(2):
                 nc.tensor.transpose(
-                    eT_ps[:, j, :], t["e_sb"][:, it, j * P : (j + 1) * P], ident_bf[:]
+                    eT_ps[:, h, :],
+                    t["e_sb"][:, it, :].bitcast(F32)[:, h * P : (h + 1) * P],
+                    ident_f32[:],
                 )
+            score_banks[u] = eT_ps
+
+        def group_scores(u):
+            if u >= UNITS:
+                return
+            b, it = divmod(u, N_TILES)
+            words = tiles[b]["e_grouped"][:].bitcast(F32)[:, it * N // 2 : (it + 1) * N // 2]
             nc.scalar.copy(
-                out=t["e_grouped"][:, it * K_PASS : (it + 1) * K_PASS].rearrange(
-                    "p (i j) -> p i j", j=PACK
-                ),
-                in_=eT_ps[:].rearrange("p j i -> p i j"),
+                out=words.rearrange("p (i h) -> p i h", h=2),
+                in_=score_banks[u][:].rearrange("p h i -> p i h"),
             )
 
         def quantise_scores(b):
@@ -238,13 +258,13 @@ def tile_self_attn_pb_kernel(tc, q, k, x, v_w, v_b, gamma, out):
             )
             tiles[b]["gain_row"] = gain_row
 
-        v_banks, v_groups, v_words, o_banks, results = {}, {}, {}, {}, {}
+        even_banks, odd_banks, odd_values, v_groups, v_words, o_banks = {}, {}, {}, {}, {}, {}
 
-        def values_matmul(n):
-            if n >= STEPS:
+        def even_matmul(i):
+            if i >= TURNS:
                 return
-            b, s = divmod(n, C_TILES)
-            cols = slice(s * P, (s + 1) * P)
+            b, r = divmod(i, ROUNDS)
+            cols = slice(PAIR * r * P, (PAIR * r + 1) * P)
             v_ps = psum.tile([P, PACK, P], F32, tag="v")
             for j in range(PACK):
                 pixels = slice(j * P, (j + 1) * P)
@@ -258,134 +278,223 @@ def tile_self_attn_pb_kernel(tc, q, k, x, v_w, v_b, gamma, out):
                         start=(g == 0),
                         stop=(g == C_PASSES - 1),
                     )
-            v_banks[n] = v_ps
+            even_banks[i] = v_ps
 
-        def add_bias(n):
-            if n >= STEPS:
+        def odd_matmul(i):
+            if i >= TURNS:
                 return
-            s = n % C_TILES
-            v_grouped = stream.tile([P, P, PACK], BF16, align_bytes=64)
+            b, r = divmod(i, ROUNDS)
+            cols = slice((PAIR * r + 1) * P, (PAIR * r + 2) * P)
+            v_ps = psum.tile([P, N], F32, tag="v")
+            for g in range(C_PASSES):
+                nc.tensor.matmul_mx(
+                    out=v_ps[:],
+                    lhsT=w_codes[:, g, cols].bitcast(FP8X4),
+                    lhsT_scale=w_scales[:, g, cols],
+                    rhs=tiles[b]["x_codes"][:, g, :].bitcast(FP8X4),
+                    rhs_scale=tiles[b]["x_scales"][:, g, :],
+                    start=(g == 0),
+                    stop=(g == C_PASSES - 1),
+                )
+            odd_banks[i] = v_ps
+
+        def even_bias(i):
+            if i >= TURNS:
+                return
             nc.vector.tensor_tensor(
-                out=v_grouped[:],
-                in0=v_banks[n][:].rearrange("p j c -> p c j"),
-                in1=bias[:, s // PAIR, s % PAIR, :].unsqueeze(2).to_broadcast([P, P, PACK]),
+                out=v_groups[i][:, 0],
+                in0=even_banks[i][:].rearrange("p j c -> p c j"),
+                in1=bias[:, i % ROUNDS, :].unsqueeze(2).to_broadcast([P, P, PACK]),
                 op=ALU.add,
             )
-            v_groups[n] = v_grouped
 
-        def quantise_values(n):
-            if n >= STEPS:
+        def odd_bias(i):
+            if i >= TURNS:
                 return
-            v_codes = stream.tile([P, P], U32, align_bytes=64)
-            v_scales = stream.tile([P, P], U8, align_bytes=64)
+            v_groups[i] = stream.tile([P, PAIR, P, PACK], BF16, name="v_grouped", align_bytes=64)
+            values = stream.tile([P, N], BF16, name="odd_values")
+            nc.scalar.activation(
+                out=values[:].rearrange("q (h p t) -> q h p t", h=2, t=2),
+                in_=odd_banks[i][:].rearrange("q (h t p) -> q h p t", h=2, t=2),
+                func=ACT.Identity,
+                bias=bias_col[:, i % ROUNDS, 1:2],
+                scale=1.0,
+            )
+            odd_values[i] = values
+
+        def odd_transpose(i):
+            if i >= TURNS:
+                return
+            vT_ps = psum.tile([P, 2, P], F32, tag="tr")
+            for h in range(2):
+                nc.tensor.transpose(
+                    vT_ps[:, h, :],
+                    odd_values[i][:].bitcast(F32)[:, h * P : (h + 1) * P],
+                    ident_f32[:],
+                )
+            odd_banks[i] = vT_ps
+
+        def odd_group(i):
+            if i >= TURNS:
+                return
+            words = v_groups[i][:, 1].rearrange("p c j -> p (c j)").bitcast(F32)
+            nc.scalar.copy(
+                out=words.rearrange("p (c h) -> p c h", h=2),
+                in_=odd_banks[i][:].rearrange("p h c -> p c h"),
+            )
+
+        def quantise_values(i):
+            v_codes = stream.tile([P, PAIR, P], U32, align_bytes=64)
+            v_scales = stream.tile([P, PAIR, P], U8, align_bytes=64)
             nc.vector.quantize_mx(
-                out=v_codes[:].bitcast(FP8X4),
-                scales=v_scales[:],
-                in_=v_groups[n][:].rearrange("p c j -> p (c j)"),
+                out=v_codes[:].rearrange("p e c -> p (e c)").bitcast(FP8X4),
+                scales=v_scales[:].rearrange("p e c -> p (e c)"),
+                in_=v_groups[i][:].rearrange("p e c j -> p (e c j)"),
             )
-            v_words[n] = (v_codes, v_scales)
+            v_words[i] = (v_codes, v_scales)
 
-        def attend_matmul(n):
-            if n < 0 or n >= STEPS:
-                return
-            b = n // C_TILES
-            v_codes, v_scales = v_words[n]
-            o_ps = psum.tile([P, N], F32, tag="o")
-            nc.tensor.matmul_mx(
-                out=o_ps[:],
-                lhsT=v_codes[:].bitcast(FP8X4),
-                lhsT_scale=v_scales[:],
-                rhs=tiles[b]["e_codes"][:].bitcast(FP8X4),
-                rhs_scale=tiles[b]["e_scales"][:],
-                start=True,
-                stop=True,
-            )
-            o_banks[n] = o_ps
+        def attend_matmul(i):
+            b = i // ROUNDS
+            v_codes, v_scales = v_words[i]
+            o_banks[i] = []
+            for e in range(PAIR):
+                o_ps = psum.tile([P, N], F32, tag="o")
+                nc.tensor.matmul_mx(
+                    out=o_ps[:],
+                    lhsT=v_codes[:, e, :].bitcast(FP8X4),
+                    lhsT_scale=v_scales[:, e, :],
+                    rhs=tiles[b]["e_codes"][:].bitcast(FP8X4),
+                    rhs_scale=tiles[b]["e_scales"][:],
+                    start=True,
+                    stop=True,
+                )
+                o_banks[i].append(o_ps)
 
-        def scale(n):
-            if n < 0 or n >= STEPS:
-                return
-            result = outs.tile([P, N], F32)
-            nc.vector.tensor_tensor(
-                out=result[:],
-                in0=o_banks[n][:],
-                in1=tiles[n // C_TILES]["gain_row"][:],
-                op=ALU.mult,
-            )
-            results[n] = result
+        def finish(i):
+            b, r = divmod(i, ROUNDS)
+            last = i == TURNS - 1
+            result = outs.tile([P, PAIR, N], F32)
+            for e in range(PAIR):
+                nc.vector.tensor_tensor(
+                    out=result[:, e, :],
+                    in0=o_banks[i][e][:],
+                    in1=tiles[b]["gain_row"][:],
+                    op=ALU.mult,
+                )
+                if last:
+                    nc.vector.tensor_tensor(
+                        out=result[:, e, :],
+                        in0=result[:, e, :],
+                        in1=x_raw[:, b, PAIR * r + e, :],
+                        op=ALU.add,
+                    )
+                    nc.sync.dma_start(out=out_view[b][:, r, e], in_=result[:, e, :])
+            if not last:
+                nc.gpsimd.tensor_tensor(
+                    out=result[:],
+                    in0=result[:],
+                    in1=x_raw[:, b, PAIR * r : PAIR * (r + 1), :],
+                    op=ALU.add,
+                )
+                nc.sync.dma_start(out=out_view[b][:, r], in_=result[:])
 
-        def add_residual(n):
-            if n < 0 or n >= STEPS:
-                return
-            b, s = divmod(n, C_TILES)
-            engine = nc.gpsimd if n < STEPS - 2 else nc.vector
-            engine.tensor_tensor(
-                out=results[n][:], in0=results[n][:], in1=x_raw[:, b, s, :], op=ALU.add
-            )
-            nc.sync.dma_start(out=out_view[b][:, s // PAIR, s % PAIR], in_=results[n][:])
-
-        def front(n):
-            values_matmul(n + 1)
-            attend_matmul(n - 1)
-            add_bias(n)
-
+        vector_copy, scalar_copy = nc.vector.tensor_copy, nc.scalar.copy
         transpose_queries(0)
+        energy_matmul(0)
+        energy_matmul(1)
+        softmax(0)
+        softmax(1)
+        regroup_x(0, vector_copy)
+        energy_matmul(2)
+        softmax(2)
+        regroup_x(1, vector_copy)
+        energy_matmul(3)
+        transpose_weights(0, 0)
+        transpose_weights(0, 1)
+        softmax(3)
+        regroup_x(2, vector_copy)
+        regroup_x(3, vector_copy)
         transpose_queries(1)
-        for u in range(N_TILES):
-            energy_matmul(u)
-            softmax(u)
+        transpose_weights(1, 0)
+        transpose_weights(1, 1)
+        group_weights(0, 0, scalar_copy)
+        group_weights(0, 1, vector_copy)
+        quantise_x(0, 0)
+        quantise_x(0, 1)
         gamma_f32 = keep.tile([P, 1], F32)
         nc.vector.tensor_copy(out=gamma_f32[:], in_=gamma_bf[:])
-        bias_ps = psum.tile([P, ROUNDS, PAIR, P], BF16, tag="tr")
+        group_weights(1, 0, scalar_copy)
+        quantise_weights(0, 0)
+        quantise_weights(0, 1)
+        bias_ps = psum.tile([P, ROUNDS, P], BF16, tag="tr")
         for r in range(ROUNDS):
-            for e in range(PAIR):
-                nc.tensor.transpose(
-                    bias_ps[:, r, e, :], bias_col[:, r, e : e + 1].to_broadcast([P, P]), ident_bf[:]
-                )
-        bias = keep.tile([P, ROUNDS, PAIR, P], BF16)
+            nc.tensor.transpose(
+                bias_ps[:, r, :], bias_col[:, r, 0:1].to_broadcast([P, P]), ident_bf[:]
+            )
+        bias = keep.tile([P, ROUNDS, P], BF16)
         nc.scalar.copy(out=bias[:], in_=bias_ps[:])
-        for u in range(N_TILES):
-            regroup_x(u, nc.vector.tensor_copy)
-        for g in range(C_PASSES):
-            quantise_x(0, g)
-        invert_sums(0)
-        for r in range(ROUNDS):
-            transpose_weights(r)
-            transpose_scores(r)
-            quantise_weights(r)
+        transpose_scores(0)
+        group_scores(0)
+        group_weights(1, 1, scalar_copy)
+        transpose_weights(2, 0)
+        transpose_weights(2, 1)
         energy_matmul(N_TILES)
-        spread_gain(0)
-        values_matmul(0)
+        transpose_scores(1)
+        odd_matmul(0)
+        group_weights(2, 0, scalar_copy)
         softmax(N_TILES)
-        quantise_scores(0)
+        odd_bias(0)
+        group_scores(1)
+        quantise_weights(1, 0)
+        quantise_weights(1, 1)
+        group_weights(2, 1, vector_copy)
+        even_matmul(0)
+        transpose_weights(3, 0)
+        transpose_weights(3, 1)
+        transpose_scores(2)
+        odd_transpose(0)
+        group_weights(3, 0, scalar_copy)
+        group_scores(2)
+        odd_group(0)
+        group_weights(3, 1, scalar_copy)
+        even_bias(0)
+        odd_matmul(1)
+        transpose_scores(3)
+        even_matmul(1)
+        energy_matmul(N_TILES + 1)
+        quantise_weights(2, 0)
+        quantise_weights(2, 1)
+        regroup_x(N_TILES, vector_copy)
+        group_scores(3)
+        invert_sums(0)
+        spread_gain(0)
+        regroup_x(N_TILES + 1, vector_copy)
+        quantise_weights(3, 0)
+        quantise_weights(3, 1)
 
-        for i in range(B * ROUNDS):
+        for i in range(TURNS):
             b, r = divmod(i, ROUNDS)
-            n = PAIR * i
-            energy_matmul(i + N_TILES + 1)
-            regroup_x(i + N_TILES, nc.scalar.copy)
-            front(n)
-            softmax(i + N_TILES + 1)
-            scale(n - 2)
-            quantise_values(n)
-            if r % 2 == 1:
-                quantise_x(b + 1, r // 2)
-            add_residual(n - 2)
-
+            quantise_values(i)
+            if r == 0:
+                quantise_scores(b)
+            if r == 1 or r == 2:
+                quantise_x(b + 1, r - 1)
             if r == ROUNDS - 1:
                 invert_sums(b + 1)
+            odd_bias(i + 1)
             transpose_scores(i + N_TILES)
+            group_scores(i + N_TILES)
+            regroup_x(i + N_TILES + 2, nc.scalar.copy)
+            attend_matmul(i)
+            odd_transpose(i + 1)
+            even_bias(i + 1)
+            odd_group(i + 1)
+            softmax(i + N_TILES + 1)
             if r == ROUNDS - 1:
                 spread_gain(b + 1)
-            if r == ROUNDS - 2:
+            if r == 1:
                 transpose_queries(b + 2)
-            front(n + 1)
-            scale(n - 1)
-            quantise_values(n + 1)
-            if r == ROUNDS - 1 and b + 1 < B:
-                quantise_scores(b + 1)
-            add_residual(n - 1)
-        attend_matmul(STEPS - 1)
-        for n in range(STEPS - 2, STEPS):
-            scale(n)
-            add_residual(n)
+            energy_matmul(i + N_TILES + 2)
+            odd_matmul(i + 2)
+            even_matmul(i + 2)
+            finish(i)

@@ -123,7 +123,7 @@ def tile_self_attn_pb_kernel(tc, q, k, x, v_w, v_b, gamma, out):
 
         tiles = {}
         energies = {}
-        score_banks = {}
+        query_banks, score_banks, gain_banks = {}, {}, {}
 
         def transpose_queries(b):
             if b >= B:
@@ -131,8 +131,13 @@ def tile_self_attn_pb_kernel(tc, q, k, x, v_w, v_b, gamma, out):
             qT_ps = psum.tile([P, N_TILES, P], BF16, tag="tr")
             for it in range(N_TILES):
                 nc.tensor.transpose(qT_ps[:, it, :], q_sb[:, b, it, :], ident_bf[:])
+            query_banks[b] = qT_ps
+
+        def halve_queries(b):
+            if b >= B:
+                return
             qT = batch.tile([P, N_TILES, P], BF16)
-            nc.scalar.mul(out=qT[:], in_=qT_ps[:], mul=0.5)
+            nc.scalar.mul(out=qT[:], in_=query_banks[b][:], mul=0.5)
             tiles[b] = {"qT": qT}
 
         def energy_matmul(u):
@@ -170,30 +175,33 @@ def tile_self_attn_pb_kernel(tc, q, k, x, v_w, v_b, gamma, out):
                 accum_out=t["row_sum"][:, it : it + 1],
             )
 
-        def transpose_scores(u):
+        def turn_bank():
+            return psum.tile([P, 2, 2, P], F32, name="turn_bank", tag="tr")
+
+        def turn(half_bank, tile):
+            for h in range(2):
+                nc.tensor.transpose(
+                    half_bank[:, h, :], tile.bitcast(F32)[:, h * P : (h + 1) * P], ident_f32[:]
+                )
+
+        def turn_scores(u, bank, half):
+            if u >= UNITS:
+                return
+            b, it = divmod(u, N_TILES)
+            score_banks[u] = bank[:, half]
+            turn(score_banks[u], tiles[b]["e_sb"][:, it, :])
+
+        def group_scores(u):
             if u >= UNITS:
                 return
             b, it = divmod(u, N_TILES)
             t = tiles[b]
             if it == 0:
                 t["e_grouped"] = batch.tile([P, N * PACK], BF16, name="e_grouped", align_bytes=64)
-            eT_ps = psum.tile([P, 2, P], F32, tag="tr")
-            for h in range(2):
-                nc.tensor.transpose(
-                    eT_ps[:, h, :],
-                    t["e_sb"][:, it, :].bitcast(F32)[:, h * P : (h + 1) * P],
-                    ident_f32[:],
-                )
-            score_banks[u] = eT_ps
-
-        def group_scores(u):
-            if u >= UNITS:
-                return
-            b, it = divmod(u, N_TILES)
-            words = tiles[b]["e_grouped"][:].bitcast(F32)[:, it * N // 2 : (it + 1) * N // 2]
+            words = t["e_grouped"][:].bitcast(F32)[:, it * N // 2 : (it + 1) * N // 2]
             nc.scalar.copy(
                 out=words.rearrange("p (i h) -> p i h", h=2),
-                in_=score_banks[u][:].rearrange("p h i -> p i h"),
+                in_=score_banks[u].rearrange("p h i -> p i h"),
             )
 
         def quantise_scores(b):
@@ -252,13 +260,19 @@ def tile_self_attn_pb_kernel(tc, q, k, x, v_w, v_b, gamma, out):
                     tiles[b]["inverse"][:, it : it + 1].to_broadcast([P, P]),
                     ident_f32[:],
                 )
+            gain_banks[b] = gain_ps
+
+        def scale_gain(b):
+            if b >= B:
+                return
             gain_row = batch.tile([P, N], F32)
             nc.scalar.activation(
-                out=gain_row[:], in_=gain_ps[:], func=ACT.Copy, scale=gamma_f32[:, 0:1]
+                out=gain_row[:], in_=gain_banks[b][:], func=ACT.Copy, scale=gamma_f32[:, 0:1]
             )
             tiles[b]["gain_row"] = gain_row
 
-        even_banks, odd_banks, odd_values, v_groups, v_words, o_banks = {}, {}, {}, {}, {}, {}
+        even_banks, odd_banks, odd_values, odd_words = {}, {}, {}, {}
+        v_groups, v_words, o_banks = {}, {}, {}
 
         def even_matmul(i):
             if i >= TURNS:
@@ -322,17 +336,11 @@ def tile_self_attn_pb_kernel(tc, q, k, x, v_w, v_b, gamma, out):
             )
             odd_values[i] = values
 
-        def odd_transpose(i):
+        def odd_turn(i, bank, half):
             if i >= TURNS:
                 return
-            vT_ps = psum.tile([P, 2, P], F32, tag="tr")
-            for h in range(2):
-                nc.tensor.transpose(
-                    vT_ps[:, h, :],
-                    odd_values[i][:].bitcast(F32)[:, h * P : (h + 1) * P],
-                    ident_f32[:],
-                )
-            odd_banks[i] = vT_ps
+            odd_words[i] = bank[:, half]
+            turn(odd_words[i], odd_values[i][:])
 
         def odd_group(i):
             if i >= TURNS:
@@ -340,7 +348,7 @@ def tile_self_attn_pb_kernel(tc, q, k, x, v_w, v_b, gamma, out):
             words = v_groups[i][:, 1].rearrange("p c j -> p (c j)").bitcast(F32)
             nc.scalar.copy(
                 out=words.rearrange("p (c h) -> p c h", h=2),
-                in_=odd_banks[i][:].rearrange("p h c -> p c h"),
+                in_=odd_words[i].rearrange("p h c -> p c h"),
             )
 
         def quantise_values(i):
@@ -400,6 +408,7 @@ def tile_self_attn_pb_kernel(tc, q, k, x, v_w, v_b, gamma, out):
 
         vector_copy, scalar_copy = nc.vector.tensor_copy, nc.scalar.copy
         transpose_queries(0)
+        halve_queries(0)
         energy_matmul(0)
         energy_matmul(1)
         softmax(0)
@@ -415,6 +424,7 @@ def tile_self_attn_pb_kernel(tc, q, k, x, v_w, v_b, gamma, out):
         regroup_x(2, vector_copy)
         regroup_x(3, vector_copy)
         transpose_queries(1)
+        halve_queries(1)
         transpose_weights(1, 0)
         transpose_weights(1, 1)
         group_weights(0, 0, scalar_copy)
@@ -433,13 +443,14 @@ def tile_self_attn_pb_kernel(tc, q, k, x, v_w, v_b, gamma, out):
             )
         bias = keep.tile([P, ROUNDS, P], BF16)
         nc.scalar.copy(out=bias[:], in_=bias_ps[:])
-        transpose_scores(0)
+        first = turn_bank()
+        turn_scores(0, first, 0)
         group_scores(0)
         group_weights(1, 1, scalar_copy)
         transpose_weights(2, 0)
         transpose_weights(2, 1)
         energy_matmul(N_TILES)
-        transpose_scores(1)
+        turn_scores(1, first, 1)
         odd_matmul(0)
         group_weights(2, 0, scalar_copy)
         softmax(N_TILES)
@@ -451,15 +462,16 @@ def tile_self_attn_pb_kernel(tc, q, k, x, v_w, v_b, gamma, out):
         even_matmul(0)
         transpose_weights(3, 0)
         transpose_weights(3, 1)
-        transpose_scores(2)
-        odd_transpose(0)
+        second = turn_bank()
+        turn_scores(2, second, 0)
+        odd_turn(0, second, 1)
         group_weights(3, 0, scalar_copy)
         group_scores(2)
         odd_group(0)
         group_weights(3, 1, scalar_copy)
         even_bias(0)
         odd_matmul(1)
-        transpose_scores(3)
+        turn_scores(3, turn_bank(), 0)
         even_matmul(1)
         energy_matmul(N_TILES + 1)
         quantise_weights(2, 0)
@@ -468,6 +480,7 @@ def tile_self_attn_pb_kernel(tc, q, k, x, v_w, v_b, gamma, out):
         group_scores(3)
         invert_sums(0)
         spread_gain(0)
+        scale_gain(0)
         regroup_x(N_TILES + 1, vector_copy)
         quantise_weights(3, 0)
         quantise_weights(3, 1)
@@ -482,19 +495,22 @@ def tile_self_attn_pb_kernel(tc, q, k, x, v_w, v_b, gamma, out):
             if r == ROUNDS - 1:
                 invert_sums(b + 1)
             odd_bias(i + 1)
-            transpose_scores(i + N_TILES)
-            group_scores(i + N_TILES)
             regroup_x(i + N_TILES + 2, nc.scalar.copy)
             attend_matmul(i)
-            odd_transpose(i + 1)
-            even_bias(i + 1)
+            bank = turn_bank()
+            odd_turn(i + 1, bank, 1)
+            turn_scores(i + N_TILES, bank, 0)
             odd_group(i + 1)
+            group_scores(i + N_TILES)
             softmax(i + N_TILES + 1)
+            energy_matmul(i + N_TILES + 2)
             if r == ROUNDS - 1:
                 spread_gain(b + 1)
+                scale_gain(b + 1)
             if r == 1:
                 transpose_queries(b + 2)
-            energy_matmul(i + N_TILES + 2)
+                halve_queries(b + 2)
+            even_bias(i + 1)
             odd_matmul(i + 2)
             even_matmul(i + 2)
             finish(i)

@@ -41,14 +41,15 @@ def tile_self_attn_pb_kernel(tc, q, k, x, v_w, v_b, gamma, out):
         outs = ctx.enter_context(tc.tile_pool(name="outs", bufs=4))
         psum = ctx.enter_context(tc.psum_pool(name="psum", bufs=2))
 
-        gamma_bf = keep.tile([P, 1], BF16)
-        nc.scalar.dma_start(out=gamma_bf[:], in_=gamma.partition_broadcast(P))
-        bias_col = keep.tile([P, ROUNDS, PAIR], BF16)
-        nc.scalar.dma_start(out=bias_col[:], in_=v_b.rearrange("(r p e) -> p r e", p=P, e=PAIR))
 
         warm = keep.tile([P, 1], F32)
         nc.vector.memset(warm[:], 0.0)
         nc.scalar.activation(out=warm[:], in_=warm[:], func=ACT.Exp)
+
+        gamma_bf = keep.tile([P, 1], BF16)
+        nc.scalar.dma_start(out=gamma_bf[:], in_=gamma.partition_broadcast(P))
+        bias_col = keep.tile([P, ROUNDS, PAIR], BF16)
+        nc.scalar.dma_start(out=bias_col[:], in_=v_b.rearrange("(r p e) -> p r e", p=P, e=PAIR))
 
         ident_bf = keep.tile([P, P], BF16)
         make_identity(nc, ident_bf[:])
@@ -137,7 +138,17 @@ def tile_self_attn_pb_kernel(tc, q, k, x, v_w, v_b, gamma, out):
             if b >= B:
                 return
             qT = batch.tile([P, N_TILES, P], BF16)
-            nc.scalar.mul(out=qT[:], in_=query_banks[b][:], mul=0.5)
+            if b == 0:
+                for part in (slice(0, 1), slice(1, N_TILES)):
+                    nc.vector.tensor_scalar(
+                        out=qT[:, part],
+                        in0=query_banks[b][:, part],
+                        scalar1=0.5,
+                        scalar2=None,
+                        op0=ALU.mult,
+                    )
+            else:
+                nc.scalar.mul(out=qT[:], in_=query_banks[b][:], mul=0.5)
             tiles[b] = {"qT": qT}
 
         def energy_matmul(u):
@@ -272,7 +283,7 @@ def tile_self_attn_pb_kernel(tc, q, k, x, v_w, v_b, gamma, out):
             tiles[b]["gain_row"] = gain_row
 
         even_banks, odd_banks, odd_values, odd_words = {}, {}, {}, {}
-        v_groups, v_words, o_banks = {}, {}, {}
+        v_groups, v_words, o_banks, results = {}, {}, {}, {}
 
         def even_matmul(i):
             if i >= TURNS:
@@ -378,33 +389,22 @@ def tile_self_attn_pb_kernel(tc, q, k, x, v_w, v_b, gamma, out):
                 )
                 o_banks[i].append(o_ps)
 
-        def finish(i):
+        def scale(i, e):
+            if i not in results:
+                results[i] = outs.tile([P, PAIR, N], F32, name="result")
+            nc.vector.tensor_tensor(
+                out=results[i][:, e, :],
+                in0=o_banks[i][e][:],
+                in1=tiles[i // ROUNDS]["gain_row"][:],
+                op=ALU.mult,
+            )
+
+        def add_residual(i, first, last, engine, queue):
             b, r = divmod(i, ROUNDS)
-            last = i == TURNS - 1
-            result = outs.tile([P, PAIR, N], F32)
-            for e in range(PAIR):
-                nc.vector.tensor_tensor(
-                    out=result[:, e, :],
-                    in0=o_banks[i][e][:],
-                    in1=tiles[b]["gain_row"][:],
-                    op=ALU.mult,
-                )
-                if last:
-                    nc.vector.tensor_tensor(
-                        out=result[:, e, :],
-                        in0=result[:, e, :],
-                        in1=x_raw[:, b, PAIR * r + e, :],
-                        op=ALU.add,
-                    )
-                    nc.sync.dma_start(out=out_view[b][:, r, e], in_=result[:, e, :])
-            if not last:
-                nc.gpsimd.tensor_tensor(
-                    out=result[:],
-                    in0=result[:],
-                    in1=x_raw[:, b, PAIR * r : PAIR * (r + 1), :],
-                    op=ALU.add,
-                )
-                nc.sync.dma_start(out=out_view[b][:, r], in_=result[:])
+            result = results[i][:, first : last + 1, :]
+            channels = slice(PAIR * r + first, PAIR * r + last + 1)
+            engine.tensor_tensor(out=result, in0=result, in1=x_raw[:, b, channels, :], op=ALU.add)
+            queue.dma_start(out=out_view[b][:, r, first : last + 1], in_=result)
 
         vector_copy, scalar_copy = nc.vector.tensor_copy, nc.scalar.copy
         transpose_queries(0)
@@ -488,6 +488,8 @@ def tile_self_attn_pb_kernel(tc, q, k, x, v_w, v_b, gamma, out):
         for i in range(TURNS):
             b, r = divmod(i, ROUNDS)
             quantise_values(i)
+            if i == TURNS - 1:
+                add_residual(i - 1, 1, 1, nc.vector, nc.scalar)
             if r == 0:
                 quantise_scores(b)
             if r == 1 or r == 2:
@@ -513,4 +515,15 @@ def tile_self_attn_pb_kernel(tc, q, k, x, v_w, v_b, gamma, out):
             even_bias(i + 1)
             odd_matmul(i + 2)
             even_matmul(i + 2)
-            finish(i)
+            if i < TURNS - 2:
+                scale(i, 0)
+                scale(i, 1)
+                add_residual(i, 0, 1, nc.gpsimd, nc.sync)
+            elif i == TURNS - 2:
+                scale(i, 1)
+                scale(i, 0)
+                add_residual(i, 0, 0, nc.gpsimd, nc.sync)
+        scale(TURNS - 1, 0)
+        scale(TURNS - 1, 1)
+        add_residual(TURNS - 1, 0, 0, nc.vector, nc.scalar)
+        add_residual(TURNS - 1, 1, 1, nc.vector, nc.sync)

@@ -414,9 +414,9 @@ def tile_self_attn_pb_kernel(tc, q, k, x, v_w, v_b, gamma, out):
         softmax(0)
         softmax(1)
         regroup_x(0, vector_copy)
+        regroup_x(1, scalar_copy)
         energy_matmul(2)
         softmax(2)
-        regroup_x(1, vector_copy)
         energy_matmul(3)
         transpose_weights(0, 0)
         transpose_weights(0, 1)
@@ -429,6 +429,7 @@ def tile_self_attn_pb_kernel(tc, q, k, x, v_w, v_b, gamma, out):
         transpose_weights(1, 1)
         group_weights(0, 0, scalar_copy)
         group_weights(0, 1, vector_copy)
+        invert_sums(0)
         quantise_x(0, 0)
         quantise_x(0, 1)
         gamma_f32 = keep.tile([P, 1], F32)
@@ -447,9 +448,9 @@ def tile_self_attn_pb_kernel(tc, q, k, x, v_w, v_b, gamma, out):
         turn_scores(0, first, 0)
         group_scores(0)
         group_weights(1, 1, scalar_copy)
+        energy_matmul(N_TILES)
         transpose_weights(2, 0)
         transpose_weights(2, 1)
-        energy_matmul(N_TILES)
         turn_scores(1, first, 1)
         odd_matmul(0)
         group_weights(2, 0, scalar_copy)
@@ -466,9 +467,11 @@ def tile_self_attn_pb_kernel(tc, q, k, x, v_w, v_b, gamma, out):
         turn_scores(2, second, 0)
         odd_turn(0, second, 1)
         group_weights(3, 0, scalar_copy)
+        spread_gain(0)
         group_scores(2)
         odd_group(0)
         group_weights(3, 1, scalar_copy)
+        scale_gain(0)
         even_bias(0)
         odd_matmul(1)
         turn_scores(3, turn_bank(), 0)
@@ -478,9 +481,6 @@ def tile_self_attn_pb_kernel(tc, q, k, x, v_w, v_b, gamma, out):
         quantise_weights(2, 1)
         regroup_x(N_TILES, vector_copy)
         group_scores(3)
-        invert_sums(0)
-        spread_gain(0)
-        scale_gain(0)
         regroup_x(N_TILES + 1, vector_copy)
         quantise_weights(3, 0)
         quantise_weights(3, 1)

from contextlib import ExitStack

import concourse.mybir as mybir
from concourse.masks import make_identity

F32 = mybir.dt.float32
BF16 = mybir.dt.bfloat16
U32 = mybir.dt.uint32
U8 = mybir.dt.uint8
FP8X4 = mybir.dt.float8_e4m3fn_x4
ACT = mybir.ActivationFunctionType
ALU = mybir.AluOpType
AX = mybir.AxisListType

B, C, D, N = 4, 1024, 128, 512
P = 128
PACK = 4
K_PASS = P * PACK
C_PASSES = C // K_PASS
C_TILES = C // P
N_TILES = N // P
PAIR = 2
ROUNDS = C_TILES // PAIR
TURNS = B * ROUNDS
UNITS = B * N_TILES

FLOPS = 2 * B * (N * N * D + C * C * N + C * N * N)


def tile_self_attn_pb_kernel(tc, q, k, x, v_w, v_b, gamma, out):
    nc = tc.nc
    x_view = x.rearrange("b (r p e) h w -> b p r e (h w)", p=P, e=PAIR)
    out_view = out.rearrange("b (r p e) h w -> b p r e (h w)", p=P, e=PAIR)
    w_view = v_w.rearrange("(r p e) k -> p r e k", p=P, e=PAIR)

    with ExitStack() as ctx:
        ctx.enter_context(tc.manual_schedule())
        keep = ctx.enter_context(tc.tile_pool(name="keep", bufs=1))
        batch = ctx.enter_context(tc.tile_pool(name="batch", bufs=2))
        stream = ctx.enter_context(tc.tile_pool(name="stream", bufs=3))
        outs = ctx.enter_context(tc.tile_pool(name="outs", bufs=4))
        psum = ctx.enter_context(tc.psum_pool(name="psum", bufs=2))


        warm = keep.tile([P, 1], F32)
        nc.vector.memset(warm[:], 0.0)
        nc.scalar.activation(out=warm[:], in_=warm[:], func=ACT.Exp)

        gamma_bf = keep.tile([P, 1], BF16)
        nc.scalar.dma_start(out=gamma_bf[:], in_=gamma.partition_broadcast(P))
        bias_col = keep.tile([P, ROUNDS, PAIR], BF16)
        nc.scalar.dma_start(out=bias_col[:], in_=v_b.rearrange("(r p e) -> p r e", p=P, e=PAIR))

        ident_bf = keep.tile([P, P], BF16)
        make_identity(nc, ident_bf[:])
        ident_f32 = keep.tile([P, P], F32)
        make_identity(nc, ident_f32[:])

        q_sb = keep.tile([P, B, N_TILES, D], BF16)
        k_sb = keep.tile([P, B, N], BF16)
        x_raw = keep.tile([P, B, C_TILES, N], BF16)
        w_raw = keep.tile([P, ROUNDS, PAIR, C], BF16)

        def load_qk(b):
            nc.sync.dma_start(out=q_sb[:, b], in_=q[b].rearrange("(t p) d -> p t d", p=P))
            nc.sync.dma_start(out=k_sb[:, b], in_=k[b])

        def load_x(b, g):
            halves = slice(2 * g, 2 * g + 2)
            nc.sync.dma_start(
                out=x_raw[:, b].rearrange("p (r e) n -> p r e n", e=PAIR)[:, halves],
                in_=x_view[b][:, halves],
            )

        def load_w(r):
            nc.sync.dma_start(out=w_raw[:, r], in_=w_view[:, r])

        load_qk(0)
        for g in range(C_PASSES):
            load_x(0, g)
        load_w(0)
        load_qk(1)
        for r in range(1, ROUNDS):
            load_w(r)
        for g in range(C_PASSES):
            load_x(1, g)
        for b in range(2, B):
            load_qk(b)
            for g in range(C_PASSES):
                load_x(b, g)

        w_grouped = keep.tile([P, C_PASSES, C * PACK], BF16, align_bytes=64)
        w_codes = keep.tile([P, C_PASSES, C], U32, align_bytes=64)
        w_scales = keep.tile([P, C_PASSES, C], U8, align_bytes=64)

        w_banks = {}

        def transpose_weights(r, g):
            w_ps = psum.tile([P, 2, PAIR, P], F32, tag="v" if g == 0 and r < ROUNDS - 1 else "o")
            for u in range(2):
                for e in range(PAIR):
                    first = (2 * g + u) * P
                    nc.tensor.transpose(
                        w_ps[:, u, e, :],
                        w_raw[:, r, e, :].bitcast(F32)[:, first : first + P],
                        ident_f32[:],
                    )
            w_banks[r, g] = w_ps

        def group_weights(r, g, copy):
            words = w_grouped[:, g, :].bitcast(F32)[:, r * N : (r + 1) * N]
            copy(
                out=words.rearrange("p (c u) -> p c u", u=2),
                in_=w_banks[r, g][:].rearrange("p u e c -> p (e c) u"),
            )

        def quantise_weights(r, g):
            cols = slice(r * PAIR * P, (r + 1) * PAIR * P)
            nc.vector.quantize_mx(
                out=w_codes[:, g, cols].bitcast(FP8X4),
                scales=w_scales[:, g, cols],
                in_=w_grouped[:, g, r * PAIR * K_PASS : (r + 1) * PAIR * K_PASS],
            )

        tiles = {}
        energies = {}
        query_banks, score_banks, gain_banks = {}, {}, {}

        def transpose_queries(b):
            if b >= B:
                return
            qT_ps = psum.tile([P, N_TILES, P], BF16, tag="tr")
            for it in range(N_TILES):
                nc.tensor.transpose(qT_ps[:, it, :], q_sb[:, b, it, :], ident_bf[:])
            query_banks[b] = qT_ps

        def halve_queries(b):
            if b >= B:
                return
            qT = batch.tile([P, N_TILES, P], BF16)
            if b == 0:
                for part in (slice(0, 1), slice(1, N_TILES)):
                    nc.vector.tensor_scalar(
                        out=qT[:, part],
                        in0=query_banks[b][:, part],
                        scalar1=0.5,
                        scalar2=None,
                        op0=ALU.mult,
                    )
            else:
                nc.scalar.mul(out=qT[:], in_=query_banks[b][:], mul=0.5)
            tiles[b] = {"qT": qT}

        def energy_matmul(u):
            if u >= UNITS:
                return
            b, it = divmod(u, N_TILES)
            energy = psum.tile([P, N], F32, tag="en")
            nc.tensor.matmul(
                energy[:], lhsT=tiles[b]["qT"][:, it, :], rhs=k_sb[:, b, :], start=True, stop=True
            )
            energies[u] = energy

        def softmax(u):
            if u >= UNITS:
                return
            b, it = divmod(u, N_TILES)
            t = tiles[b]
            if it == 0:
                t["neg_max"] = batch.tile([P, N_TILES], F32, name="neg_max")
                t["row_sum"] = batch.tile([P, N_TILES], F32, name="row_sum")
                t["e_sb"] = batch.tile([P, N_TILES, N], BF16, name="e_sb")
            nc.vector.tensor_reduce(
                out=t["neg_max"][:, it : it + 1],
                in_=energies[u][:],
                axis=AX.X,
                op=ALU.max,
                negate=True,
            )
            nc.scalar.activation(
                out=t["e_sb"][:, it, :].rearrange("q (u p e) -> q u p e", u=2, e=2),
                in_=energies[u][:].rearrange("q (u e p) -> q u p e", u=2, e=2),
                func=ACT.Exp,
                bias=t["neg_max"][:, it : it + 1],
                scale=1.0,
                accum_out=t["row_sum"][:, it : it + 1],
            )

        def turn_bank():
            return psum.tile([P, 2, 2, P], F32, name="turn_bank", tag="tr")

        def turn(half_bank, tile):
            for h in range(2):
                nc.tensor.transpose(
                    half_bank[:, h, :], tile.bitcast(F32)[:, h * P : (h + 1) * P], ident_f32[:]
                )

        def turn_scores(u, bank, half):
            if u >= UNITS:
                return
            b, it = divmod(u, N_TILES)
            score_banks[u] = bank[:, half]
            turn(score_banks[u], tiles[b]["e_sb"][:, it, :])

        def group_scores(u):
            if u >= UNITS:
                return
            b, it = divmod(u, N_TILES)
            t = tiles[b]
            if it == 0:
                t["e_grouped"] = batch.tile([P, N * PACK], BF16, name="e_grouped", align_bytes=64)
            words = t["e_grouped"][:].bitcast(F32)[:, it * N // 2 : (it + 1) * N // 2]
            nc.scalar.copy(
                out=words.rearrange("p (i h) -> p i h", h=2),
                in_=score_banks[u].rearrange("p h i -> p i h"),
            )

        def quantise_scores(b):
            t = tiles[b]
            t["e_codes"] = batch.tile([P, N], U32, name="e_codes", align_bytes=64)
            t["e_scales"] = batch.tile([P, N], U8, name="e_scales", align_bytes=64)
            nc.vector.quantize_mx(
                out=t["e_codes"][:].bitcast(FP8X4), scales=t["e_scales"][:], in_=t["e_grouped"][:]
            )

        def regroup_x(u, copy):
            if u >= UNITS:
                return
            b, piece = divmod(u, N_TILES)
            t = tiles[b]
            if piece == 0:
                t["x_grouped"] = batch.tile(
                    [P, C_PASSES, N * PACK], BF16, name="x_grouped", align_bytes=64
                )
                t["x_codes"] = batch.tile([P, C_PASSES, N], U32, name="x_codes", align_bytes=64)
                t["x_scales"] = batch.tile([P, C_PASSES, N], U8, name="x_scales", align_bytes=64)
            g, half = divmod(piece, 2)
            pixels = slice(half * (N // 2), (half + 1) * (N // 2))
            grouped = t["x_grouped"][:, g, half * N * 2 : (half + 1) * N * 2]
            copy(
                out=grouped.rearrange("p (c i t) -> p c t i", i=4, t=PACK),
                in_=x_raw[:, b, g * PACK : (g + 1) * PACK, pixels].rearrange(
                    "p t (c i) -> p c t i", i=4
                ),
            )

        def quantise_x(b, g):
            if b >= B:
                return
            t = tiles[b]
            nc.vector.quantize_mx(
                out=t["x_codes"][:, g, :].bitcast(FP8X4),
                scales=t["x_scales"][:, g, :],
                in_=t["x_grouped"][:, g, :],
            )

        def invert_sums(b):
            if b >= B:
                return
            inverse = batch.tile([P, N_TILES], F32)
            nc.vector.reciprocal(out=inverse[:], in_=tiles[b]["row_sum"][:])
            tiles[b]["inverse"] = inverse

        def spread_gain(b):
            if b >= B:
                return
            gain_ps = psum.tile([P, N], F32, tag="tr")
            for it in range(N_TILES):
                nc.tensor.transpose(
                    gain_ps[:, it * P : (it + 1) * P],
                    tiles[b]["inverse"][:, it : it + 1].to_broadcast([P, P]),
                    ident_f32[:],
                )
            gain_banks[b] = gain_ps

        def scale_gain(b):
            if b >= B:
                return
            gain_row = batch.tile([P, N], F32)
            nc.scalar.activation(
                out=gain_row[:], in_=gain_banks[b][:], func=ACT.Copy, scale=gamma_f32[:, 0:1]
            )
            tiles[b]["gain_row"] = gain_row

        even_banks, odd_banks, odd_values, odd_words = {}, {}, {}, {}
        v_groups, v_words, o_banks, results = {}, {}, {}, {}

        def even_matmul(i):
            if i >= TURNS:
                return
            b, r = divmod(i, ROUNDS)
            cols = slice(PAIR * r * P, (PAIR * r + 1) * P)
            v_ps = psum.tile([P, PACK, P], F32, tag="v")
            for j in range(PACK):
                pixels = slice(j * P, (j + 1) * P)
                for g in range(C_PASSES):
                    nc.tensor.matmul_mx(
                        out=v_ps[:, j, :],
                        lhsT=tiles[b]["x_codes"][:, g, pixels].bitcast(FP8X4),
                        lhsT_scale=tiles[b]["x_scales"][:, g, pixels],
                        rhs=w_codes[:, g, cols].bitcast(FP8X4),
                        rhs_scale=w_scales[:, g, cols],
                        start=(g == 0),
                        stop=(g == C_PASSES - 1),
                    )
            even_banks[i] = v_ps

        def odd_matmul(i):
            if i >= TURNS:
                return
            b, r = divmod(i, ROUNDS)
            cols = slice((PAIR * r + 1) * P, (PAIR * r + 2) * P)
            v_ps = psum.tile([P, N], F32, tag="v")
            for g in range(C_PASSES):
                nc.tensor.matmul_mx(
                    out=v_ps[:],
                    lhsT=w_codes[:, g, cols].bitcast(FP8X4),
                    lhsT_scale=w_scales[:, g, cols],
                    rhs=tiles[b]["x_codes"][:, g, :].bitcast(FP8X4),
                    rhs_scale=tiles[b]["x_scales"][:, g, :],
                    start=(g == 0),
                    stop=(g == C_PASSES - 1),
                )
            odd_banks[i] = v_ps

        def even_bias(i):
            if i >= TURNS:
                return
            nc.vector.tensor_tensor(
                out=v_groups[i][:, 0],
                in0=even_banks[i][:].rearrange("p j c -> p c j"),
                in1=bias[:, i % ROUNDS, :].unsqueeze(2).to_broadcast([P, P, PACK]),
                op=ALU.add,
            )

        def odd_bias(i):
            if i >= TURNS:
                return
            v_groups[i] = stream.tile([P, PAIR, P, PACK], BF16, name="v_grouped", align_bytes=64)
            values = stream.tile([P, N], BF16, name="odd_values")
            nc.scalar.activation(
                out=values[:].rearrange("q (h p t) -> q h p t", h=2, t=2),
                in_=odd_banks[i][:].rearrange("q (h t p) -> q h p t", h=2, t=2),
                func=ACT.Identity,
                bias=bias_col[:, i % ROUNDS, 1:2],
                scale=1.0,
            )
            odd_values[i] = values

        def odd_turn(i, bank, half):
            if i >= TURNS:
                return
            odd_words[i] = bank[:, half]
            turn(odd_words[i], odd_values[i][:])

        def odd_group(i):
            if i >= TURNS:
                return
            words = v_groups[i][:, 1].rearrange("p c j -> p (c j)").bitcast(F32)
            nc.scalar.copy(
                out=words.rearrange("p (c h) -> p c h", h=2),
                in_=odd_words[i].rearrange("p h c -> p c h"),
            )

        def quantise_values(i):
            v_codes = stream.tile([P, PAIR, P], U32, align_bytes=64)
            v_scales = stream.tile([P, PAIR, P], U8, align_bytes=64)
            nc.vector.quantize_mx(
                out=v_codes[:].rearrange("p e c -> p (e c)").bitcast(FP8X4),
                scales=v_scales[:].rearrange("p e c -> p (e c)"),
                in_=v_groups[i][:].rearrange("p e c j -> p (e c j)"),
            )
            v_words[i] = (v_codes, v_scales)

        def attend_matmul(i):
            b = i // ROUNDS
            v_codes, v_scales = v_words[i]
            o_banks[i] = []
            for e in range(PAIR):
                o_ps = psum.tile([P, N], F32, tag="o")
                nc.tensor.matmul_mx(
                    out=o_ps[:],
                    lhsT=v_codes[:, e, :].bitcast(FP8X4),
                    lhsT_scale=v_scales[:, e, :],
                    rhs=tiles[b]["e_codes"][:].bitcast(FP8X4),
                    rhs_scale=tiles[b]["e_scales"][:],
                    start=True,
                    stop=True,
                )
                o_banks[i].append(o_ps)

        def scale(i, e):
            if i not in results:
                results[i] = outs.tile([P, PAIR, N], F32, name="result")
            nc.vector.tensor_tensor(
                out=results[i][:, e, :],
                in0=o_banks[i][e][:],
                in1=tiles[i // ROUNDS]["gain_row"][:],
                op=ALU.mult,
            )

        def add_residual(i, first, last, engine, queue):
            b, r = divmod(i, ROUNDS)
            result = results[i][:, first : last + 1, :]
            channels = slice(PAIR * r + first, PAIR * r + last + 1)
            engine.tensor_tensor(out=result, in0=result, in1=x_raw[:, b, channels, :], op=ALU.add)
            queue.dma_start(out=out_view[b][:, r, first : last + 1], in_=result)

        vector_copy, scalar_copy = nc.vector.tensor_copy, nc.scalar.copy
        transpose_queries(0)
        halve_queries(0)
        energy_matmul(0)
        energy_matmul(1)
        softmax(0)
        softmax(1)
        regroup_x(0, vector_copy)
        regroup_x(1, scalar_copy)
        energy_matmul(2)
        softmax(2)
        energy_matmul(3)
        transpose_weights(0, 0)
        transpose_weights(0, 1)
        softmax(3)
        regroup_x(2, vector_copy)
        regroup_x(3, vector_copy)
        transpose_queries(1)
        halve_queries(1)
        transpose_weights(1, 0)
        transpose_weights(1, 1)
        group_weights(0, 0, scalar_copy)
        group_weights(0, 1, vector_copy)
        invert_sums(0)
        quantise_x(0, 0)
        quantise_x(0, 1)
        gamma_f32 = keep.tile([P, 1], F32)
        nc.vector.tensor_copy(out=gamma_f32[:], in_=gamma_bf[:])
        group_weights(1, 0, scalar_copy)
        quantise_weights(0, 0)
        quantise_weights(0, 1)
        bias_ps = psum.tile([P, ROUNDS, P], BF16, tag="tr")
        for r in range(ROUNDS):
            nc.tensor.transpose(
                bias_ps[:, r, :], bias_col[:, r, 0:1].to_broadcast([P, P]), ident_bf[:]
            )
        bias = keep.tile([P, ROUNDS, P], BF16)
        nc.scalar.copy(out=bias[:], in_=bias_ps[:])
        first = turn_bank()
        turn_scores(0, first, 0)
        group_scores(0)
        group_weights(1, 1, scalar_copy)
        energy_matmul(N_TILES)
        transpose_weights(2, 0)
        transpose_weights(2, 1)
        turn_scores(1, first, 1)
        odd_matmul(0)
        group_weights(2, 0, scalar_copy)
        softmax(N_TILES)
        odd_bias(0)
        group_scores(1)
        quantise_weights(1, 0)
        quantise_weights(1, 1)
        group_weights(2, 1, vector_copy)
        even_matmul(0)
        transpose_weights(3, 0)
        transpose_weights(3, 1)
        second = turn_bank()
        turn_scores(2, second, 0)
        odd_turn(0, second, 1)
        group_weights(3, 0, scalar_copy)
        spread_gain(0)
        group_scores(2)
        odd_group(0)
        group_weights(3, 1, scalar_copy)
        scale_gain(0)
        even_bias(0)
        odd_matmul(1)
        turn_scores(3, turn_bank(), 0)
        even_matmul(1)
        energy_matmul(N_TILES + 1)
        quantise_weights(2, 0)
        quantise_weights(2, 1)
        regroup_x(N_TILES, vector_copy)
        group_scores(3)
        regroup_x(N_TILES + 1, vector_copy)
        quantise_weights(3, 0)
        quantise_weights(3, 1)

        for i in range(TURNS):
            b, r = divmod(i, ROUNDS)
            quantise_values(i)
            if i == TURNS - 1:
                add_residual(i - 1, 1, 1, nc.vector, nc.scalar)
            if r == 0:
                quantise_scores(b)
            if r == 1 or r == 2:
                quantise_x(b + 1, r - 1)
            if r == ROUNDS - 1:
                invert_sums(b + 1)
            odd_bias(i + 1)
            regroup_x(i + N_TILES + 2, nc.scalar.copy)
            attend_matmul(i)
            bank = turn_bank()
            odd_turn(i + 1, bank, 1)
            turn_scores(i + N_TILES, bank, 0)
            odd_group(i + 1)
            group_scores(i + N_TILES)
            softmax(i + N_TILES + 1)
            energy_matmul(i + N_TILES + 2)
            if r == ROUNDS - 1:
                spread_gain(b + 1)
                scale_gain(b + 1)
            if r == 1:
                transpose_queries(b + 2)
                halve_queries(b + 2)
            even_bias(i + 1)
            odd_matmul(i + 2)
            even_matmul(i + 2)
            if i < TURNS - 2:
                scale(i, 0)
                scale(i, 1)
                add_residual(i, 0, 1, nc.gpsimd, nc.sync)
            elif i == TURNS - 2:
                scale(i, 1)
                scale(i, 0)
                add_residual(i, 0, 0, nc.gpsimd, nc.sync)
        scale(TURNS - 1, 0)
        scale(TURNS - 1, 1)
        add_residual(TURNS - 1, 0, 0, nc.vector, nc.scalar)
        add_residual(TURNS - 1, 1, 1, nc.vector, nc.sync)
